import numpy as np
import ml_dtypes


def mxq(x, axis, fmt="e4m3"):
    dtype, down = {"e4m3": (ml_dtypes.float8_e4m3fn, 7), "e5m2": (ml_dtypes.float8_e5m2, 14)}[fmt]
    v = np.moveaxis(np.asarray(x, np.float32).astype(ml_dtypes.bfloat16).astype(np.float64), axis, -1)
    blocks = v.reshape(v.shape[:-1] + (-1, 32))
    amax = np.abs(blocks).max(-1, keepdims=True)
    byte = np.maximum(np.where(amax > 0, np.frexp(amax)[1] - 1 + 127, 0) - down, 1)
    scale = np.exp2(byte - 127.0)
    codes = (blocks / scale).astype(np.float32).astype(dtype).astype(np.float64)
    return np.moveaxis((codes * scale).reshape(v.shape), -1, axis)


WIDE = False


def mx_kscale(k):
    if not WIDE:
        return np.ones(k)
    levels = np.array([10, -10, 5, -5, 0])
    a = np.random.permutation(np.resize(levels, k // 512 * 4)).reshape(k // 512, 4)
    idx = np.arange(k)
    return np.exp2(a[idx // 512, idx % 128 // 32])


BF16 = ml_dtypes.bfloat16


def bf(x):
    return np.asarray(x, np.float32).astype(BF16)


def f64(x):
    return np.asarray(x).astype(np.float64)


B, IN, H = 4096, 512, 512


def sigmoid(v):
    return 1.0 / (1.0 + np.exp(-v))


def setup_inputs():
    s, u = mx_kscale(IN), mx_kscale(H)
    return {'input': bf(np.random.standard_normal((B, IN)) * s),
            'state': bf(np.random.standard_normal((B, H)) * u),
            'W1': bf(np.random.standard_normal((IN, H)) * 0.7 / np.sqrt(IN) / s[:, None]),
            'W3': bf(np.random.standard_normal((IN, H)) * 0.7 / np.sqrt(IN) / s[:, None]),
            'U1': bf(np.random.standard_normal((H, H)) * 0.7 / np.sqrt(H) / u[:, None]),
            'U3': bf(np.random.standard_normal((H, H)) * 1.0 / np.sqrt(H) / u[:, None]),
            'bias_r': bf(np.random.standard_normal((1, H)) * 0.5),
            'bias_update': bf(np.random.standard_normal((1, H)) * 0.5)}


def reference(input, state, W1, W3, U1, U3, bias_r, bias_update):
    h = f64(state)
    xq = mxq(f64(input), 1, 'e4m3')
    hq = mxq(h, 1, 'e4m3')
    wComp1 = xq @ mxq(f64(W1), 0, 'e4m3')
    wComp3 = xq @ mxq(f64(W3), 0, 'e4m3')
    uComp1 = hq @ mxq(f64(U1), 0, 'e4m3')
    r = sigmoid(wComp1 + uComp1 + f64(bias_r))
    return np.tanh(wComp3 + (mxq(r * h, 1, 'e4m3') @ mxq(f64(U3), 0, 'e4m3')) + f64(bias_update))

@@ -1,0 +1,217 @@
+from contextlib import ExitStack
+
+import concourse.mybir as mybir
+from concourse.masks import make_identity
+
+F32 = mybir.dt.float32
+BF16 = mybir.dt.bfloat16
+U32 = mybir.dt.uint32
+U8 = mybir.dt.uint8
+FP8X4 = mybir.dt.float8_e4m3fn_x4
+ACT = mybir.ActivationFunctionType
+ALU = mybir.AluOpType
+
+P = 128
+ROWS = 4096
+FEAT = 512
+TILES = ROWS // P
+GT = 4
+G = TILES // GT
+GC = GT * P
+FLOPS = 4 * 2 * ROWS * FEAT * FEAT
+
+LAG = 1
+MANUAL = False
+
+
+def tile_grulrcell_pa_t_kernel(tc, x_in, h_in, w1, w3, u1, u3, bias_r, bias_u, out):
+    nc = tc.nc
+    with ExitStack() as ctx:
+        const = ctx.enter_context(tc.tile_pool(name="const", bufs=1))
+        work = ctx.enter_context(tc.tile_pool(name="work", bufs=2))
+        tpool = ctx.enter_context(tc.psum_pool(name="tpool", bufs=2))
+        m1pool = ctx.enter_context(tc.psum_pool(name="m1pool", bufs=3))
+        m2pool = ctx.enter_context(tc.psum_pool(name="m2pool", bufs=3))
+        if MANUAL:
+            ctx.enter_context(tc.manual_schedule())
+
+        x_v = x_in.rearrange("(p t) k -> p t k", t=TILES)
+        h_v = h_in.rearrange("(p t) k -> p t k", t=TILES)
+        o_v = out.rearrange("(p t) n -> p t n", t=TILES)
+
+        raw = {}
+        nat = {}
+
+        def load_w(key, src):
+            t = const.tile([P, 4, FEAT], BF16, name="raw_" + key, tag="raw_" + key)
+            nc.sync.dma_start(
+                out=t[:].rearrange("q (u e) n -> q u (e n)", u=2),
+                in_=src.rearrange("(u q e) n -> q u (e n)", u=2, e=2),
+            )
+            raw[key] = t
+
+        def load_a(key, view, g):
+            t = const.tile([P, GT * FEAT], BF16, name="nat_%s%d" % (key, g), tag="nat_%s%d" % (key, g))
+            nc.sync.dma_start(
+                out=t[:].rearrange("p (j k) -> p j k", j=GT),
+                in_=view[:, g * GT:(g + 1) * GT, :],
+            )
+            nat[(key, g)] = t
+
+        load_w("w1", w1)
+        load_a("x", x_v, 0)
+        load_w("u1", u1)
+        load_a("h", h_v, 0)
+        load_a("x", x_v, 1)
+        load_a("h", h_v, 1)
+        load_w("w3", w3)
+        load_w("u3", u3)
+        for g in range(2, G):
+            load_a("x", x_v, g)
+            load_a("h", h_v, g)
+
+        ident = const.tile([P, P], F32, name="ident", tag="ident")
+        make_identity(nc, ident[:])
+
+        brb = const.tile([P, 4], BF16, name="brb", tag="brb")
+        nc.scalar.dma_start(
+            out=brb[:].rearrange("q (u e) -> q u e", u=2),
+            in_=bias_r.rearrange("o (u q e) -> q (o u) e", u=2, e=2),
+        )
+        br = const.tile([P, 4], F32, name="br", tag="br")
+        nc.vector.tensor_copy(out=br[:], in_=brb[:])
+
+        bz = const.tile([P, FEAT], BF16, name="bz", tag="bz")
+        nc.gpsimd.memset(bz[:], 0.0)
+        nc.scalar.dma_start(out=bz[0:1, :], in_=bias_u)
+        ones = const.tile([P, P], BF16, name="ones", tag="ones")
+        nc.gpsimd.memset(ones[:], 1.0)
+        bu = const.tile([P, FEAT], F32, name="bu", tag="bu")
+
+        def prep_bias_u():
+            ps = m2pool.tile([P, FEAT], F32, name="bu_ps", tag="m2")
+            nc.tensor.matmul(out=ps[:], lhsT=ones[:], rhs=bz[:], start=True, stop=True)
+            nc.vector.tensor_copy(out=bu[:], in_=ps[:])
+
+        wc = {}
+        ws = {}
+
+        def prep_w(key, stationary):
+            wg = work.tile([P, 4 * FEAT], BF16, name="wg_" + key, tag="wg", align_bytes=64)
+            if stationary:
+                src = raw[key][:].rearrange("q t (u m e) -> q t u m e", u=2, e=2)
+                for tq in range(4):
+                    uu, ee = divmod(tq, 2)
+                    nc.vector.tensor_copy(
+                        out=wg[:, tq * 512:(tq + 1) * 512].rearrange("q (m t) -> q m t", t=4),
+                        in_=src[:, :, uu, :, ee].rearrange("q t m -> q m t"),
+                    )
+            else:
+                nc.vector.tensor_copy(
+                    out=wg[:].rearrange("q (n t) -> q n t", t=4),
+                    in_=raw[key][:].rearrange("q t n -> q n t"),
+                )
+            c = const.tile([P, FEAT], U32, name="wc_" + key, tag="wc_" + key, align_bytes=64)
+            s = const.tile([P, FEAT], U8, name="ws_" + key, tag="ws_" + key, align_bytes=64)
+            nc.vector.quantize_mx(out=c[:].bitcast(FP8X4), scales=s[:], in_=wg[:])
+            wc[key] = c
+            ws[key] = s
+
+        grp = {}
+        codes = {}
+        planes = {}
+
+        def transpose_group(key, g):
+            natw = nat[(key, g)][:].bitcast(F32)
+            gt = work.tile([P, 4 * GC], BF16, name="g_%s%d" % (key, g), tag="g_" + key, bufs=3, align_bytes=64)
+            gw = gt[:].bitcast(F32).rearrange("q (c u) -> q c u", u=2)
+            for hf in range(2):
+                tp = tpool.tile([P, 2, 2 * P], F32, name="tp_%s%d_%d" % (key, g, hf), tag="tp")
+                for jj in range(2):
+                    j = 2 * hf + jj
+                    for u in range(2):
+                        nc.tensor.transpose(
+                            tp[:, u, jj * P:(jj + 1) * P],
+                            natw[:, j * 256 + u * P:j * 256 + (u + 1) * P],
+                            ident[:],
+                        )
+                nc.scalar.copy(
+                    out=gw[:, hf * 2 * P:(hf + 1) * 2 * P, :],
+                    in_=tp[:].rearrange("q u c -> q c u"),
+                )
+            grp[(key, g)] = gt
+
+        def quantise(key, g, src, resident):
+            if resident:
+                c = const.tile([P, GC], U32, name="c_%s%d" % (key, g), tag="c_%s%d" % (key, g), align_bytes=64)
+                s = const.tile([P, GC], U8, name="s_%s%d" % (key, g), tag="s_%s%d" % (key, g), align_bytes=64)
+            else:
+                c = work.tile([P, GC], U32, name="c_%s%d" % (key, g), tag="c_" + key, align_bytes=64)
+                s = work.tile([P, GC], U8, name="s_%s%d" % (key, g), tag="s_" + key, align_bytes=64)
+            nc.vector.quantize_mx(out=c[:].bitcast(FP8X4), scales=s[:], in_=src[:])
+            codes[(key, g)] = c
+            planes[(key, g)] = s
+
+        def stage1(g):
+            r = work.tile([P, 4, GC], F32, name="r%d" % g, tag="r")
+            for t in range(4):
+                cols = slice(t * P, (t + 1) * P)
+                acc = m1pool.tile([P, GC], F32, name="m1_%d_%d" % (g, t), tag="m1")
+                nc.tensor.matmul_mx(
+                    out=acc[:],
+                    lhsT=wc["w1"][:, cols].bitcast(FP8X4), lhsT_scale=ws["w1"][:, cols],
+                    rhs=codes[("x", g)][:].bitcast(FP8X4), rhs_scale=planes[("x", g)][:],
+                    start=True, stop=False,
+                )
+                nc.tensor.matmul_mx(
+                    out=acc[:],
+                    lhsT=wc["u1"][:, cols].bitcast(FP8X4), lhsT_scale=ws["u1"][:, cols],
+                    rhs=codes[("h", g)][:].bitcast(FP8X4), rhs_scale=planes[("h", g)][:],
+                    start=False, stop=True,
+                )
+                nc.scalar.activation(out=r[:, t, :], in_=acc[:], func=ACT.Sigmoid, bias=br[:, t:t + 1], scale=1.0)
+            rh = work.tile([P, 4 * GC], BF16, name="rh%d" % g, tag="rh", align_bytes=64)
+            nc.vector.tensor_tensor(
+                out=rh[:].rearrange("q (c t) -> q c t", t=4),
+                in0=r[:].rearrange("q t c -> q c t"),
+                in1=grp[("h", g)][:].rearrange("q (c t) -> q c t", t=4),
+                op=ALU.mult,
+            )
+            quantise("rh", g, rh, True)
+
+        def stage2(g):
+            o = work.tile([P, GT, FEAT], F32, name="o%d" % g, tag="o", bufs=3)
+            for j in range(GT):
+                cols = slice(j * P, (j + 1) * P)
+                acc = m2pool.tile([P, FEAT], F32, name="m2_%d_%d" % (g, j), tag="m2")
+                nc.tensor.matmul_mx(
+                    out=acc[:],
+                    lhsT=codes[("x", g)][:, cols].bitcast(FP8X4), lhsT_scale=planes[("x", g)][:, cols],
+                    rhs=wc["w3"][:].bitcast(FP8X4), rhs_scale=ws["w3"][:],
+                    start=True, stop=False,
+                )
+                nc.tensor.matmul_mx(
+                    out=acc[:],
+                    lhsT=codes[("rh", g)][:, cols].bitcast(FP8X4), lhsT_scale=planes[("rh", g)][:, cols],
+                    rhs=wc["u3"][:].bitcast(FP8X4), rhs_scale=ws["u3"][:],
+                    start=False, stop=True,
+                )
+                nc.vector.tensor_tensor(out=o[:, j, :], in0=acc[:], in1=bu[:], op=ALU.add)
+            nc.scalar.activation(out=o[:], in_=o[:], func=ACT.Tanh)
+            nc.sync.dma_start(out=o_v[:, g * GT:(g + 1) * GT, :], in_=o[:])
+
+        prep_w("w1", True)
+        prep_w("u1", True)
+        for step in range(G + LAG):
+            if step < G:
+                transpose_group("x", step)
+                transpose_group("h", step)
+                quantise("x", step, grp[("x", step)], True)
+                quantise("h", step, grp[("h", step)], False)
+                stage1(step)
+            if step == 0:
+                prep_w("w3", False)
+                prep_w("u3", False)
+                prep_bias_u()
+            if step >= LAG:
+                stage2(step - LAG)

@@ -20,8 +20,11 @@ G = TILES // GT
 GC = GT * P
 FLOPS = 4 * 2 * ROWS * FEAT * FEAT
 
-LAG = 1
-MANUAL = False
+LEAD = 2
+NAT_BUFS = 5
+FIRST_EARLY = 2
+FINE_LAST = 2
+BANKS = ("m2", "m2", "tp", "tp", "tp", "m1", "m1", "m1")
 
 
 def tile_grulrcell_pa_t_kernel(tc, x_in, h_in, w1, w3, u1, u3, bias_r, bias_u, out):
@@ -29,18 +32,28 @@ def tile_grulrcell_pa_t_kernel(tc, x_in, h_in, w1, w3, u1, u3, bias_r, bias_u, o
     with ExitStack() as ctx:
         const = ctx.enter_context(tc.tile_pool(name="const", bufs=1))
         work = ctx.enter_context(tc.tile_pool(name="work", bufs=2))
-        tpool = ctx.enter_context(tc.psum_pool(name="tpool", bufs=2))
-        m1pool = ctx.enter_context(tc.psum_pool(name="m1pool", bufs=3))
-        m2pool = ctx.enter_context(tc.psum_pool(name="m2pool", bufs=3))
-        if MANUAL:
-            ctx.enter_context(tc.manual_schedule())
+        psum = {
+            "tp": ctx.enter_context(tc.psum_pool(name="tpool", bufs=3)),
+            "m1": ctx.enter_context(tc.psum_pool(name="m1pool", bufs=3)),
+            "m2": ctx.enter_context(tc.psum_pool(name="m2pool", bufs=2)),
+        }
+        ctx.enter_context(tc.manual_schedule())
 
-        x_v = x_in.rearrange("(p t) k -> p t k", t=TILES)
-        h_v = h_in.rearrange("(p t) k -> p t k", t=TILES)
+        views = {
+            "x": x_in.rearrange("(p t) k -> p t k", t=TILES),
+            "h": h_in.rearrange("(p t) k -> p t k", t=TILES),
+        }
         o_v = out.rearrange("(p t) n -> p t n", t=TILES)
 
         raw = {}
         nat = {}
+        wc = {}
+        ws = {}
+        grp = {}
+        codes = {}
+        planes = {}
+        r_of = {}
+        o_of = {}
 
         def load_w(key, src):
             t = const.tile([P, 4, FEAT], BF16, name="raw_" + key, tag="raw_" + key)
@@ -50,66 +63,25 @@ def tile_grulrcell_pa_t_kernel(tc, x_in, h_in, w1, w3, u1, u3, bias_r, bias_u, o
             )
             raw[key] = t
 
-        def load_a(key, view, g):
-            t = const.tile([P, GT * FEAT], BF16, name="nat_%s%d" % (key, g), tag="nat_%s%d" % (key, g))
+        def load_a(key, g):
+            t = work.tile([P, GT * FEAT], BF16, name="nat_%s%d" % (key, g), tag="nat_" + key, bufs=NAT_BUFS)
             nc.sync.dma_start(
                 out=t[:].rearrange("p (j k) -> p j k", j=GT),
-                in_=view[:, g * GT:(g + 1) * GT, :],
+                in_=views[key][:, g * GT:(g + 1) * GT, :],
             )
             nat[(key, g)] = t
-
-        load_w("w1", w1)
-        load_a("x", x_v, 0)
-        load_w("u1", u1)
-        load_a("h", h_v, 0)
-        load_a("x", x_v, 1)
-        load_a("h", h_v, 1)
-        load_w("w3", w3)
-        load_w("u3", u3)
-        for g in range(2, G):
-            load_a("x", x_v, g)
-            load_a("h", h_v, g)
-
-        ident = const.tile([P, P], F32, name="ident", tag="ident")
-        make_identity(nc, ident[:])
-
-        brb = const.tile([P, 4], BF16, name="brb", tag="brb")
-        nc.scalar.dma_start(
-            out=brb[:].rearrange("q (u e) -> q u e", u=2),
-            in_=bias_r.rearrange("o (u q e) -> q (o u) e", u=2, e=2),
-        )
-        br = const.tile([P, 4], F32, name="br", tag="br")
-        nc.vector.tensor_copy(out=br[:], in_=brb[:])
-
-        bz = const.tile([P, FEAT], BF16, name="bz", tag="bz")
-        nc.gpsimd.memset(bz[:], 0.0)
-        nc.scalar.dma_start(out=bz[0:1, :], in_=bias_u)
-        ones = const.tile([P, P], BF16, name="ones", tag="ones")
-        nc.gpsimd.memset(ones[:], 1.0)
-        bu = const.tile([P, FEAT], F32, name="bu", tag="bu")
-
-        def prep_bias_u():
-            ps = m2pool.tile([P, FEAT], F32, name="bu_ps", tag="m2")
-            nc.tensor.matmul(out=ps[:], lhsT=ones[:], rhs=bz[:], start=True, stop=True)
-            nc.vector.tensor_copy(out=bu[:], in_=ps[:])
-
-        wc = {}
-        ws = {}
 
         def prep_w(key, stationary):
             wg = work.tile([P, 4 * FEAT], BF16, name="wg_" + key, tag="wg", align_bytes=64)
             if stationary:
-                src = raw[key][:].rearrange("q t (u m e) -> q t u m e", u=2, e=2)
-                for tq in range(4):
-                    uu, ee = divmod(tq, 2)
-                    nc.vector.tensor_copy(
-                        out=wg[:, tq * 512:(tq + 1) * 512].rearrange("q (m t) -> q m t", t=4),
-                        in_=src[:, :, uu, :, ee].rearrange("q t m -> q m t"),
-                    )
+                src = raw[key][:].rearrange("q t (u m e) -> q u e m t", u=2, e=2)
+                dst = wg[:].rearrange("q (u e m t) -> q u e m t", u=2, e=2, t=4)
+                for uu in range(2):
+                    nc.vector.tensor_copy(out=dst[:, uu], in_=src[:, uu])
             else:
                 nc.vector.tensor_copy(
-                    out=wg[:].rearrange("q (n t) -> q n t", t=4),
-                    in_=raw[key][:].rearrange("q t n -> q n t"),
+                    out=wg[:].rearrange("q (c i t) -> q c t i", i=4, t=4),
+                    in_=raw[key][:].rearrange("q t (c i) -> q c t i", i=4),
                 )
             c = const.tile([P, FEAT], U32, name="wc_" + key, tag="wc_" + key, align_bytes=64)
             s = const.tile([P, FEAT], U8, name="ws_" + key, tag="ws_" + key, align_bytes=64)
@@ -117,46 +89,48 @@ def tile_grulrcell_pa_t_kernel(tc, x_in, h_in, w1, w3, u1, u3, bias_r, bias_u, o
             wc[key] = c
             ws[key] = s
 
-        grp = {}
-        codes = {}
-        planes = {}
-
-        def transpose_group(key, g):
-            natw = nat[(key, g)][:].bitcast(F32)
-            gt = work.tile([P, 4 * GC], BF16, name="g_%s%d" % (key, g), tag="g_" + key, bufs=3, align_bytes=64)
-            gw = gt[:].bitcast(F32).rearrange("q (c u) -> q c u", u=2)
-            for hf in range(2):
-                tp = tpool.tile([P, 2, 2 * P], F32, name="tp_%s%d_%d" % (key, g, hf), tag="tp")
-                for jj in range(2):
-                    j = 2 * hf + jj
-                    for u in range(2):
-                        nc.tensor.transpose(
-                            tp[:, u, jj * P:(jj + 1) * P],
-                            natw[:, j * 256 + u * P:j * 256 + (u + 1) * P],
-                            ident[:],
-                        )
-                nc.scalar.copy(
-                    out=gw[:, hf * 2 * P:(hf + 1) * 2 * P, :],
-                    in_=tp[:].rearrange("q u c -> q c u"),
-                )
-            grp[(key, g)] = gt
-
         def quantise(key, g, src, resident):
             if resident:
                 c = const.tile([P, GC], U32, name="c_%s%d" % (key, g), tag="c_%s%d" % (key, g), align_bytes=64)
                 s = const.tile([P, GC], U8, name="s_%s%d" % (key, g), tag="s_%s%d" % (key, g), align_bytes=64)
             else:
-                c = work.tile([P, GC], U32, name="c_%s%d" % (key, g), tag="c_" + key, align_bytes=64)
-                s = work.tile([P, GC], U8, name="s_%s%d" % (key, g), tag="s_" + key, align_bytes=64)
+                c = work.tile([P, GC], U32, name="c_%s%d" % (key, g), tag="c_" + key, bufs=3, align_bytes=64)
+                s = work.tile([P, GC], U8, name="s_%s%d" % (key, g), tag="s_" + key, bufs=3, align_bytes=64)
             nc.vector.quantize_mx(out=c[:].bitcast(FP8X4), scales=s[:], in_=src[:])
             codes[(key, g)] = c
             planes[(key, g)] = s
 
-        def stage1(g):
+        def front(g):
+            for key, bufs in (("x", 3), ("h", 4)):
+                natw = nat[(key, g)][:].bitcast(F32)
+                gt = work.tile([P, 4 * GC], BF16, name="g_%s%d" % (key, g), tag="g_" + key, bufs=bufs, align_bytes=64)
+                gw = gt[:].bitcast(F32).rearrange("q (c u) -> q c u", u=2)
+                for hf in range(2):
+                    tp = psum["tp"].tile([P, 2, 2 * P], F32, name="tp_%s%d_%d" % (key, g, hf), tag="tp")
+                    for jj in range(2):
+                        j = 2 * hf + jj
+                        for u in range(2):
+                            nc.tensor.transpose(
+                                tp[:, u, jj * P:(jj + 1) * P],
+                                natw[:, j * 256 + u * P:j * 256 + (u + 1) * P],
+                                ident[:],
+                            )
+                    nc.scalar.copy(
+                        out=gw[:, hf * 2 * P:(hf + 1) * 2 * P, :],
+                        in_=tp[:].rearrange("q u c -> q c u"),
+                    )
+                grp[(key, g)] = gt
+            quantise("x", g, grp[("x", g)], True)
+            quantise("h", g, grp[("h", g)], False)
+            if g + NAT_BUFS < G:
+                load_a("x", g + NAT_BUFS)
+                load_a("h", g + NAT_BUFS)
+
+        def gate(g):
             r = work.tile([P, 4, GC], F32, name="r%d" % g, tag="r")
             for t in range(4):
                 cols = slice(t * P, (t + 1) * P)
-                acc = m1pool.tile([P, GC], F32, name="m1_%d_%d" % (g, t), tag="m1")
+                acc = psum["m1"].tile([P, GC], F32, name="m1_%d_%d" % (g, t), tag="m1")
                 nc.tensor.matmul_mx(
                     out=acc[:],
                     lhsT=wc["w1"][:, cols].bitcast(FP8X4), lhsT_scale=ws["w1"][:, cols],
@@ -170,48 +144,98 @@ def tile_grulrcell_pa_t_kernel(tc, x_in, h_in, w1, w3, u1, u3, bias_r, bias_u, o
                     start=False, stop=True,
                 )
                 nc.scalar.activation(out=r[:, t, :], in_=acc[:], func=ACT.Sigmoid, bias=br[:, t:t + 1], scale=1.0)
+            r_of[g] = r
+
+        def reset_state(g):
             rh = work.tile([P, 4 * GC], BF16, name="rh%d" % g, tag="rh", align_bytes=64)
             nc.vector.tensor_tensor(
                 out=rh[:].rearrange("q (c t) -> q c t", t=4),
-                in0=r[:].rearrange("q t c -> q c t"),
+                in0=r_of[g][:].rearrange("q t c -> q c t"),
                 in1=grp[("h", g)][:].rearrange("q (c t) -> q c t", t=4),
                 op=ALU.mult,
             )
             quantise("rh", g, rh, True)
 
-        def stage2(g):
-            o = work.tile([P, GT, FEAT], F32, name="o%d" % g, tag="o", bufs=3)
-            for j in range(GT):
-                cols = slice(j * P, (j + 1) * P)
-                acc = m2pool.tile([P, FEAT], F32, name="m2_%d_%d" % (g, j), tag="m2")
-                nc.tensor.matmul_mx(
-                    out=acc[:],
-                    lhsT=codes[("x", g)][:, cols].bitcast(FP8X4), lhsT_scale=planes[("x", g)][:, cols],
-                    rhs=wc["w3"][:].bitcast(FP8X4), rhs_scale=ws["w3"][:],
-                    start=True, stop=False,
-                )
-                nc.tensor.matmul_mx(
-                    out=acc[:],
-                    lhsT=codes[("rh", g)][:, cols].bitcast(FP8X4), lhsT_scale=planes[("rh", g)][:, cols],
-                    rhs=wc["u3"][:].bitcast(FP8X4), rhs_scale=ws["u3"][:],
-                    start=False, stop=True,
-                )
-                nc.vector.tensor_tensor(out=o[:, j, :], in0=acc[:], in1=bu[:], op=ALU.add)
-            nc.scalar.activation(out=o[:], in_=o[:], func=ACT.Tanh)
-            nc.sync.dma_start(out=o_v[:, g * GT:(g + 1) * GT, :], in_=o[:])
+        def candidate_sum(i, bank):
+            g, j = divmod(i, GT)
+            if j == 0:
+                o_of[g] = work.tile([P, GT, FEAT], F32, name="o%d" % g, tag="o", bufs=4)
+            cols = slice(j * P, (j + 1) * P)
+            acc = psum[bank].tile([P, FEAT], F32, name="m2_%d" % i, tag=bank)
+            nc.tensor.matmul_mx(
+                out=acc[:],
+                lhsT=codes[("x", g)][:, cols].bitcast(FP8X4), lhsT_scale=planes[("x", g)][:, cols],
+                rhs=wc["w3"][:].bitcast(FP8X4), rhs_scale=ws["w3"][:],
+                start=True, stop=False,
+            )
+            nc.tensor.matmul_mx(
+                out=acc[:],
+                lhsT=codes[("rh", g)][:, cols].bitcast(FP8X4), lhsT_scale=planes[("rh", g)][:, cols],
+                rhs=wc["u3"][:].bitcast(FP8X4), rhs_scale=ws["u3"][:],
+                start=False, stop=True,
+            )
+            nc.vector.tensor_tensor(out=o_of[g][:, j, :], in0=acc[:], in1=bu[:], op=ALU.add)
+
+        def finish(i):
+            g, j = divmod(i, GT)
+            o = o_of[g]
+            nc.scalar.activation(out=o[:, j, :], in_=o[:, j, :], func=ACT.Tanh)
+            if i >= TILES - FINE_LAST:
+                nc.sync.dma_start(out=o_v[:, i:i + 1, :], in_=o[:, j:j + 1, :])
+            elif j % 2 == 1:
+                nc.sync.dma_start(out=o_v[:, i - 1:i + 1, :], in_=o[:, j - 1:j + 1, :])
+
+        brb = const.tile([P, 4], BF16, name="brb", tag="brb")
+        nc.scalar.dma_start(
+            out=brb[:].rearrange("q (u e) -> q u e", u=2),
+            in_=bias_r.rearrange("o (u q e) -> q (o u) e", u=2, e=2),
+        )
+        bz = const.tile([P, FEAT], BF16, name="bz", tag="bz")
+        nc.gpsimd.memset(bz[:], 0.0)
+        nc.scalar.dma_start(out=bz[0:1, :], in_=bias_u)
+        ident = const.tile([P, P], F32, name="ident", tag="ident")
+        make_identity(nc, ident[:])
+        ones = const.tile([P, P], BF16, name="ones", tag="ones")
+        nc.gpsimd.memset(ones[:], 1.0)
+        bu = const.tile([P, FEAT], F32, name="bu", tag="bu")
+
+        load_w("w1", w1)
+        load_a("x", 0)
+        load_w("u1", u1)
+        load_a("h", 0)
+        load_a("x", 1)
+        load_a("h", 1)
+        load_w("w3", w3)
+        load_w("u3", u3)
+        for g in range(2, NAT_BUFS):
+            load_a("x", g)
+            load_a("h", g)
 
         prep_w("w1", True)
+        br = const.tile([P, 4], F32, name="br", tag="br")
+        nc.vector.tensor_copy(out=br[:], in_=brb[:])
         prep_w("u1", True)
-        for step in range(G + LAG):
-            if step < G:
-                transpose_group("x", step)
-                transpose_group("h", step)
-                quantise("x", step, grp[("x", step)], True)
-                quantise("h", step, grp[("h", step)], False)
-                stage1(step)
-            if step == 0:
+        for g in range(LEAD):
+            front(g)
+        early = 0
+        for n in range(G):
+            gate(n)
+            if n == 0:
+                bu_ps = psum["m2"].tile([P, FEAT], F32, name="bu_ps", tag="m2")
+                nc.tensor.matmul(out=bu_ps[:], lhsT=ones[:], rhs=bz[:], start=True, stop=True)
+                nc.scalar.copy(out=bu[:], in_=bu_ps[:])
                 prep_w("w3", False)
                 prep_w("u3", False)
-                prep_bias_u()
-            if step >= LAG:
-                stage2(step - LAG)
+            if n >= 1:
+                reset_state(n - 1)
+            if n >= FIRST_EARLY:
+                candidate_sum(early, "m2")
+                early += 1
+            if n + LEAD < G:
+                front(n + LEAD)
+        reset_state(G - 1)
+        for i in range(early):
+            finish(i)
+        for i in range(early, TILES):
+            candidate_sum(i, BANKS[(i - early) % len(BANKS)])
+            finish(i)

@@ -46,6 +46,8 @@ def tile_grulrcell_pa_t_kernel(tc, x_in, h_in, w1, w3, u1, u3, bias_r, bias_u, o
         o_v = out.rearrange("(p t) n -> p t n", t=TILES)
 
         raw = {}
+        wgs = {}
+        rh_of = {}
         nat = {}
         wc = {}
         ws = {}
@@ -63,15 +65,17 @@ def tile_grulrcell_pa_t_kernel(tc, x_in, h_in, w1, w3, u1, u3, bias_r, bias_u, o
             )
             raw[key] = t
 
-        def load_a(key, g):
+        def load_a(key, g, pieces=1):
             t = work.tile([P, GT * FEAT], BF16, name="nat_%s%d" % (key, g), tag="nat_" + key, bufs=NAT_BUFS)
-            nc.sync.dma_start(
-                out=t[:].rearrange("p (j k) -> p j k", j=GT),
-                in_=views[key][:, g * GT:(g + 1) * GT, :],
-            )
+            n = GT // pieces
+            for i in range(pieces):
+                nc.sync.dma_start(
+                    out=t[:, i * n * FEAT:(i + 1) * n * FEAT].rearrange("p (j k) -> p j k", j=n),
+                    in_=views[key][:, g * GT + i * n:g * GT + (i + 1) * n, :],
+                )
             nat[(key, g)] = t
 
-        def prep_w(key, stationary):
+        def regroup_w(key, stationary):
             wg = work.tile([P, 4 * FEAT], BF16, name="wg_" + key, tag="wg", align_bytes=64)
             if stationary:
                 src = raw[key][:].rearrange("q t (u m e) -> q u e m t", u=2, e=2)
@@ -83,9 +87,18 @@ def tile_grulrcell_pa_t_kernel(tc, x_in, h_in, w1, w3, u1, u3, bias_r, bias_u, o
                     out=wg[:].rearrange("q (c i t) -> q c t i", i=4, t=4),
                     in_=raw[key][:].rearrange("q t (c i) -> q c t i", i=4),
                 )
+            wgs[key] = wg
+
+        def quantise_w(key, pieces):
             c = const.tile([P, FEAT], U32, name="wc_" + key, tag="wc_" + key, align_bytes=64)
             s = const.tile([P, FEAT], U8, name="ws_" + key, tag="ws_" + key, align_bytes=64)
-            nc.vector.quantize_mx(out=c[:].bitcast(FP8X4), scales=s[:], in_=wg[:])
+            w = FEAT // pieces
+            for i in range(pieces):
+                nc.vector.quantize_mx(
+                    out=c[:, i * w:(i + 1) * w].bitcast(FP8X4),
+                    scales=s[:, i * w:(i + 1) * w],
+                    in_=wgs[key][:, 4 * i * w:4 * (i + 1) * w],
+                )
             wc[key] = c
             ws[key] = s
 
@@ -154,7 +167,7 @@ def tile_grulrcell_pa_t_kernel(tc, x_in, h_in, w1, w3, u1, u3, bias_r, bias_u, o
                 in1=grp[("h", g)][:].rearrange("q (c t) -> q c t", t=4),
                 op=ALU.mult,
             )
-            quantise("rh", g, rh, True)
+            rh_of[g] = rh
 
         def candidate_sum(i, bank):
             g, j = divmod(i, GT)
@@ -200,9 +213,9 @@ def tile_grulrcell_pa_t_kernel(tc, x_in, h_in, w1, w3, u1, u3, bias_r, bias_u, o
         bu = const.tile([P, FEAT], F32, name="bu", tag="bu")
 
         load_w("w1", w1)
-        load_a("x", 0)
+        load_a("x", 0, 2)
         load_w("u1", u1)
-        load_a("h", 0)
+        load_a("h", 0, 2)
         load_a("x", 1)
         load_a("h", 1)
         load_w("w3", w3)
@@ -211,10 +224,12 @@ def tile_grulrcell_pa_t_kernel(tc, x_in, h_in, w1, w3, u1, u3, bias_r, bias_u, o
             load_a("x", g)
             load_a("h", g)
 
-        prep_w("w1", True)
+        regroup_w("w1", True)
+        quantise_w("w1", 2)
         br = const.tile([P, 4], F32, name="br", tag="br")
         nc.vector.tensor_copy(out=br[:], in_=brb[:])
-        prep_w("u1", True)
+        regroup_w("u1", True)
+        quantise_w("u1", 2)
         for g in range(LEAD):
             front(g)
         early = 0
@@ -224,13 +239,17 @@ def tile_grulrcell_pa_t_kernel(tc, x_in, h_in, w1, w3, u1, u3, bias_r, bias_u, o
                 bu_ps = psum["m2"].tile([P, FEAT], F32, name="bu_ps", tag="m2")
                 nc.tensor.matmul(out=bu_ps[:], lhsT=ones[:], rhs=bz[:], start=True, stop=True)
                 nc.scalar.copy(out=bu[:], in_=bu_ps[:])
-                prep_w("w3", False)
-                prep_w("u3", False)
+                regroup_w("w3", False)
+                regroup_w("u3", False)
+                quantise_w("w3", 1)
+                quantise_w("u3", 1)
             if n >= 1:
                 reset_state(n - 1)
             if n >= FIRST_EARLY:
                 candidate_sum(early, "m2")
                 early += 1
+            if n >= 1:
+                quantise("rh", n - 1, rh_of[n - 1], True)
             if n + LEAD < G:
                 front(n + LEAD)
         reset_state(G - 1)
@@ -238,4 +257,6 @@ def tile_grulrcell_pa_t_kernel(tc, x_in, h_in, w1, w3, u1, u3, bias_r, bias_u, o
             finish(i)
         for i in range(early, TILES):
             candidate_sum(i, BANKS[(i - early) % len(BANKS)])
+            if i == early:
+                quantise("rh", G - 1, rh_of[G - 1], True)
             finish(i)

@@ -24,6 +24,9 @@ LEAD = 2
 NAT_BUFS = 5
 FIRST_EARLY = 2
 FINE_LAST = 2
+POOL_FROM = 6
+POOL_PIECES = 4
+LATE_EVERY = 8
 BANKS = ("m2", "m2", "tp", "tp", "tp", "m1", "m1", "m1")
 
 
@@ -160,13 +163,17 @@ def tile_grulrcell_pa_t_kernel(tc, x_in, h_in, w1, w3, u1, u3, bias_r, bias_u, o
             r_of[g] = r
 
         def reset_state(g):
-            rh = work.tile([P, 4 * GC], BF16, name="rh%d" % g, tag="rh", align_bytes=64)
-            nc.vector.tensor_tensor(
-                out=rh[:].rearrange("q (c t) -> q c t", t=4),
-                in0=r_of[g][:].rearrange("q t c -> q c t"),
-                in1=grp[("h", g)][:].rearrange("q (c t) -> q c t", t=4),
-                op=ALU.mult,
-            )
+            rh = work.tile([P, 4 * GC], BF16, name="rh%d" % g, tag="rh", bufs=3, align_bytes=64)
+            dst = rh[:].rearrange("q (c t) -> q c t", t=4)
+            gate_v = r_of[g][:].rearrange("q t c -> q c t")
+            state_v = grp[("h", g)][:].rearrange("q (c t) -> q c t", t=4)
+            if g < POOL_FROM:
+                nc.vector.tensor_tensor(out=dst, in0=gate_v, in1=state_v, op=ALU.mult)
+            else:
+                w = GC // POOL_PIECES
+                for i in range(POOL_PIECES):
+                    cs = slice(i * w, (i + 1) * w)
+                    nc.gpsimd.tensor_tensor(out=dst[:, cs, :], in0=gate_v[:, cs, :], in1=state_v[:, cs, :], op=ALU.mult)
             rh_of[g] = rh
 
         def candidate_sum(i, bank):
@@ -243,20 +250,22 @@ def tile_grulrcell_pa_t_kernel(tc, x_in, h_in, w1, w3, u1, u3, bias_r, bias_u, o
                 regroup_w("u3", False)
                 quantise_w("w3", 1)
                 quantise_w("u3", 1)
-            if n >= 1:
+            if n >= POOL_FROM:
+                reset_state(n)
+            if 1 <= n <= POOL_FROM:
                 reset_state(n - 1)
             if n >= FIRST_EARLY:
                 candidate_sum(early, "m2")
                 early += 1
-            if n >= 1:
+            if 1 <= n <= POOL_FROM:
                 quantise("rh", n - 1, rh_of[n - 1], True)
             if n + LEAD < G:
                 front(n + LEAD)
-        reset_state(G - 1)
         for i in range(early):
             finish(i)
         for i in range(early, TILES):
             candidate_sum(i, BANKS[(i - early) % len(BANKS)])
-            if i == early:
-                quantise("rh", G - 1, rh_of[G - 1], True)
+            late, rest = divmod(i - early + 1, LATE_EVERY)
+            if rest == 0 and POOL_FROM + late - 1 < G:
+                quantise("rh", POOL_FROM + late - 1, rh_of[POOL_FROM + late - 1], True)
             finish(i)

@@ -24,9 +24,6 @@ LEAD = 2
 NAT_BUFS = 5
 FIRST_EARLY = 2
 FINE_LAST = 2
-POOL_FROM = 6
-POOL_PIECES = 4
-LATE_EVERY = 8
 BANKS = ("m2", "m2", "tp", "tp", "tp", "m1", "m1", "m1")
 
 
@@ -163,17 +160,13 @@ def tile_grulrcell_pa_t_kernel(tc, x_in, h_in, w1, w3, u1, u3, bias_r, bias_u, o
             r_of[g] = r
 
         def reset_state(g):
-            rh = work.tile([P, 4 * GC], BF16, name="rh%d" % g, tag="rh", bufs=3, align_bytes=64)
-            dst = rh[:].rearrange("q (c t) -> q c t", t=4)
-            gate_v = r_of[g][:].rearrange("q t c -> q c t")
-            state_v = grp[("h", g)][:].rearrange("q (c t) -> q c t", t=4)
-            if g < POOL_FROM:
-                nc.vector.tensor_tensor(out=dst, in0=gate_v, in1=state_v, op=ALU.mult)
-            else:
-                w = GC // POOL_PIECES
-                for i in range(POOL_PIECES):
-                    cs = slice(i * w, (i + 1) * w)
-                    nc.gpsimd.tensor_tensor(out=dst[:, cs, :], in0=gate_v[:, cs, :], in1=state_v[:, cs, :], op=ALU.mult)
+            rh = work.tile([P, 4 * GC], BF16, name="rh%d" % g, tag="rh", align_bytes=64)
+            nc.vector.tensor_tensor(
+                out=rh[:].rearrange("q (b i t) -> q b t i", i=4, t=4),
+                in0=r_of[g][:].rearrange("q t (b i) -> q b t i", i=4),
+                in1=grp[("h", g)][:].rearrange("q (b i t) -> q b t i", i=4, t=4),
+                op=ALU.mult,
+            )
             rh_of[g] = rh
 
         def candidate_sum(i, bank):
@@ -250,22 +243,20 @@ def tile_grulrcell_pa_t_kernel(tc, x_in, h_in, w1, w3, u1, u3, bias_r, bias_u, o
                 regroup_w("u3", False)
                 quantise_w("w3", 1)
                 quantise_w("u3", 1)
-            if n >= POOL_FROM:
-                reset_state(n)
-            if 1 <= n <= POOL_FROM:
+            if n >= 1:
                 reset_state(n - 1)
             if n >= FIRST_EARLY:
                 candidate_sum(early, "m2")
                 early += 1
-            if 1 <= n <= POOL_FROM:
+            if n >= 1:
                 quantise("rh", n - 1, rh_of[n - 1], True)
             if n + LEAD < G:
                 front(n + LEAD)
+        reset_state(G - 1)
         for i in range(early):
             finish(i)
         for i in range(early, TILES):
             candidate_sum(i, BANKS[(i - early) % len(BANKS)])
-            late, rest = divmod(i - early + 1, LATE_EVERY)
-            if rest == 0 and POOL_FROM + late - 1 < G:
-                quantise("rh", POOL_FROM + late - 1, rh_of[POOL_FROM + late - 1], True)
+            if i == early:
+                quantise("rh", G - 1, rh_of[G - 1], True)
             finish(i)

@@ -12,251 +12,253 @@ ACT = mybir.ActivationFunctionType
 ALU = mybir.AluOpType
 
 P = 128
+PACK = 4
 ROWS = 4096
 FEAT = 512
 TILES = ROWS // P
-GT = 4
-G = TILES // GT
-GC = GT * P
+GROUP_TILES = 4
+GROUPS = TILES // GROUP_TILES
+GROUP_ROWS = GROUP_TILES * P
+CHUNKS = FEAT // P
+WORDS = FEAT // 2
 FLOPS = 4 * 2 * ROWS * FEAT * FEAT
 
 LEAD = 2
-NAT_BUFS = 5
-FIRST_EARLY = 2
-FINE_LAST = 2
-BANKS = ("m2", "m2", "tp", "tp", "tp", "m1", "m1", "m1")
+LOADS_AHEAD = 4
+FIRST_FILLED = 2
+SINGLE_STORES = 2
+BANKS = {"transposes": 3, "gate": 3, "candidate": 2}
+TURNS = ("candidate",) * 2 + ("transposes",) * 3 + ("gate",) * 3
 
 
 def tile_grulrcell_pa_t_kernel(tc, x_in, h_in, w1, w3, u1, u3, bias_r, bias_u, out):
     nc = tc.nc
     with ExitStack() as ctx:
-        const = ctx.enter_context(tc.tile_pool(name="const", bufs=1))
+        keep = ctx.enter_context(tc.tile_pool(name="keep", bufs=1))
         work = ctx.enter_context(tc.tile_pool(name="work", bufs=2))
-        psum = {
-            "tp": ctx.enter_context(tc.psum_pool(name="tpool", bufs=3)),
-            "m1": ctx.enter_context(tc.psum_pool(name="m1pool", bufs=3)),
-            "m2": ctx.enter_context(tc.psum_pool(name="m2pool", bufs=2)),
-        }
+        psum = {}
+        for role in BANKS:
+            psum[role] = ctx.enter_context(tc.psum_pool(name=role, bufs=BANKS[role]))
         ctx.enter_context(tc.manual_schedule())
 
-        views = {
+        rows_of = {
             "x": x_in.rearrange("(p t) k -> p t k", t=TILES),
             "h": h_in.rearrange("(p t) k -> p t k", t=TILES),
         }
-        o_v = out.rearrange("(p t) n -> p t n", t=TILES)
+        out_rows = out.rearrange("(p t) n -> p t n", t=TILES)
 
-        raw = {}
-        wgs = {}
-        rh_of = {}
-        nat = {}
-        wc = {}
-        ws = {}
-        grp = {}
-        codes = {}
-        planes = {}
-        r_of = {}
-        o_of = {}
+        w_loaded = {}
+        w_grouped = {}
+        w_codes = {}
+        w_scales = {}
+        loaded = {}
+        acts = {}
+        act_codes = {}
+        act_scales = {}
+        gates = {}
+        resets = {}
+        reset_codes = {}
+        reset_scales = {}
+        results = {}
 
-        def load_w(key, src):
-            t = const.tile([P, 4, FEAT], BF16, name="raw_" + key, tag="raw_" + key)
+        def load_weight(key, src):
+            t = keep.tile([P, PACK, FEAT], BF16, name="w_loaded_" + key)
             nc.sync.dma_start(
                 out=t[:].rearrange("q (u e) n -> q u (e n)", u=2),
                 in_=src.rearrange("(u q e) n -> q u (e n)", u=2, e=2),
             )
-            raw[key] = t
+            w_loaded[key] = t
 
-        def load_a(key, g, pieces=1):
-            t = work.tile([P, GT * FEAT], BF16, name="nat_%s%d" % (key, g), tag="nat_" + key, bufs=NAT_BUFS)
-            n = GT // pieces
+        def load_rows(key, g, pieces=1):
+            t = work.tile([P, GROUP_TILES * FEAT], BF16, name="loaded_%s%d" % (key, g), tag="loaded_" + key,
+                          bufs=LOADS_AHEAD)
+            n = GROUP_TILES // pieces
             for i in range(pieces):
                 nc.sync.dma_start(
                     out=t[:, i * n * FEAT:(i + 1) * n * FEAT].rearrange("p (j k) -> p j k", j=n),
-                    in_=views[key][:, g * GT + i * n:g * GT + (i + 1) * n, :],
+                    in_=rows_of[key][:, g * GROUP_TILES + i * n:g * GROUP_TILES + (i + 1) * n, :],
                 )
-            nat[(key, g)] = t
+            loaded[(key, g)] = t
 
-        def regroup_w(key, stationary):
-            wg = work.tile([P, 4 * FEAT], BF16, name="wg_" + key, tag="wg", align_bytes=64)
+        def regroup_weight(key, stationary):
+            grouped = work.tile([P, PACK * FEAT], BF16, name="w_grouped_" + key, tag="w_grouped", align_bytes=64)
             if stationary:
-                src = raw[key][:].rearrange("q t (u m e) -> q u e m t", u=2, e=2)
-                dst = wg[:].rearrange("q (u e m t) -> q u e m t", u=2, e=2, t=4)
-                for uu in range(2):
-                    nc.vector.tensor_copy(out=dst[:, uu], in_=src[:, uu])
+                src = w_loaded[key][:].rearrange("q t (u m e) -> q u e m t", u=2, e=2)
+                dst = grouped[:].rearrange("q (u e m t) -> q u e m t", u=2, e=2, t=PACK)
+                for u in range(2):
+                    nc.vector.tensor_copy(out=dst[:, u], in_=src[:, u])
             else:
                 nc.vector.tensor_copy(
-                    out=wg[:].rearrange("q (c i t) -> q c t i", i=4, t=4),
-                    in_=raw[key][:].rearrange("q t (c i) -> q c t i", i=4),
+                    out=grouped[:].rearrange("q (c i t) -> q c t i", i=4, t=PACK),
+                    in_=w_loaded[key][:].rearrange("q t (c i) -> q c t i", i=4),
                 )
-            wgs[key] = wg
+            w_grouped[key] = grouped
 
-        def quantise_w(key, pieces):
-            c = const.tile([P, FEAT], U32, name="wc_" + key, tag="wc_" + key, align_bytes=64)
-            s = const.tile([P, FEAT], U8, name="ws_" + key, tag="ws_" + key, align_bytes=64)
-            w = FEAT // pieces
+        def quantise_weight(key, pieces):
+            codes = keep.tile([P, FEAT], U32, name="w_codes_" + key, align_bytes=64)
+            scales = keep.tile([P, FEAT], U8, name="w_scales_" + key, align_bytes=64)
+            n = FEAT // pieces
             for i in range(pieces):
                 nc.vector.quantize_mx(
-                    out=c[:, i * w:(i + 1) * w].bitcast(FP8X4),
-                    scales=s[:, i * w:(i + 1) * w],
-                    in_=wgs[key][:, 4 * i * w:4 * (i + 1) * w],
+                    out=codes[:, i * n:(i + 1) * n].bitcast(FP8X4),
+                    scales=scales[:, i * n:(i + 1) * n],
+                    in_=w_grouped[key][:, PACK * i * n:PACK * (i + 1) * n],
                 )
-            wc[key] = c
-            ws[key] = s
+            w_codes[key] = codes
+            w_scales[key] = scales
 
-        def quantise(key, g, src, resident):
-            if resident:
-                c = const.tile([P, GC], U32, name="c_%s%d" % (key, g), tag="c_%s%d" % (key, g), align_bytes=64)
-                s = const.tile([P, GC], U8, name="s_%s%d" % (key, g), tag="s_%s%d" % (key, g), align_bytes=64)
-            else:
-                c = work.tile([P, GC], U32, name="c_%s%d" % (key, g), tag="c_" + key, bufs=3, align_bytes=64)
-                s = work.tile([P, GC], U8, name="s_%s%d" % (key, g), tag="s_" + key, bufs=3, align_bytes=64)
-            nc.vector.quantize_mx(out=c[:].bitcast(FP8X4), scales=s[:], in_=src[:])
-            codes[(key, g)] = c
-            planes[(key, g)] = s
-
-        def front(g):
-            for key, bufs in (("x", 3), ("h", 4)):
-                natw = nat[(key, g)][:].bitcast(F32)
-                gt = work.tile([P, 4 * GC], BF16, name="g_%s%d" % (key, g), tag="g_" + key, bufs=bufs, align_bytes=64)
-                gw = gt[:].bitcast(F32).rearrange("q (c u) -> q c u", u=2)
-                for hf in range(2):
-                    tp = psum["tp"].tile([P, 2, 2 * P], F32, name="tp_%s%d_%d" % (key, g, hf), tag="tp")
-                    for jj in range(2):
-                        j = 2 * hf + jj
+        def transpose_group(g):
+            grouped = work.tile([P, 2 * PACK * GROUP_ROWS], BF16, name="acts%d" % g, tag="acts", bufs=LEAD + 2,
+                                align_bytes=64)
+            words = grouped[:].bitcast(F32).rearrange("q (o b r u) -> q o b r u", o=2, b=2, u=2)
+            for o, key in enumerate(("x", "h")):
+                src = loaded[(key, g)][:].bitcast(F32)
+                for b in range(2):
+                    bank = psum["transposes"].tile([P, 2, 2 * P], F32, name="t_%s%d_%d" % (key, g, b),
+                                                   tag="transposes")
+                    for j in range(2):
+                        first = (2 * b + j) * WORDS
                         for u in range(2):
                             nc.tensor.transpose(
-                                tp[:, u, jj * P:(jj + 1) * P],
-                                natw[:, j * 256 + u * P:j * 256 + (u + 1) * P],
-                                ident[:],
+                                bank[:, u, j * P:(j + 1) * P],
+                                src[:, first + u * P:first + (u + 1) * P],
+                                identity[:],
                             )
-                    nc.scalar.copy(
-                        out=gw[:, hf * 2 * P:(hf + 1) * 2 * P, :],
-                        in_=tp[:].rearrange("q u c -> q c u"),
-                    )
-                grp[(key, g)] = gt
-            quantise("x", g, grp[("x", g)], True)
-            quantise("h", g, grp[("h", g)], False)
-            if g + NAT_BUFS < G:
-                load_a("x", g + NAT_BUFS)
-                load_a("h", g + NAT_BUFS)
+                    nc.scalar.copy(out=words[:, o, b], in_=bank[:].rearrange("q u r -> q r u"))
+            codes = keep.tile([P, 2 * GROUP_ROWS], U32, name="act_codes%d" % g, align_bytes=64)
+            scales = keep.tile([P, 2 * GROUP_ROWS], U8, name="act_scales%d" % g, align_bytes=64)
+            nc.vector.quantize_mx(out=codes[:].bitcast(FP8X4), scales=scales[:], in_=grouped[:])
+            acts[g] = grouped
+            act_codes[g] = codes
+            act_scales[g] = scales
+            if g + LOADS_AHEAD < GROUPS:
+                load_rows("x", g + LOADS_AHEAD)
+                load_rows("h", g + LOADS_AHEAD)
 
         def gate(g):
-            r = work.tile([P, 4, GC], F32, name="r%d" % g, tag="r")
-            for t in range(4):
+            r = work.tile([P, CHUNKS, GROUP_ROWS], F32, name="gate%d" % g, tag="gate")
+            for t in range(CHUNKS):
                 cols = slice(t * P, (t + 1) * P)
-                acc = psum["m1"].tile([P, GC], F32, name="m1_%d_%d" % (g, t), tag="m1")
-                nc.tensor.matmul_mx(
-                    out=acc[:],
-                    lhsT=wc["w1"][:, cols].bitcast(FP8X4), lhsT_scale=ws["w1"][:, cols],
-                    rhs=codes[("x", g)][:].bitcast(FP8X4), rhs_scale=planes[("x", g)][:],
-                    start=True, stop=False,
-                )
-                nc.tensor.matmul_mx(
-                    out=acc[:],
-                    lhsT=wc["u1"][:, cols].bitcast(FP8X4), lhsT_scale=ws["u1"][:, cols],
-                    rhs=codes[("h", g)][:].bitcast(FP8X4), rhs_scale=planes[("h", g)][:],
-                    start=False, stop=True,
-                )
-                nc.scalar.activation(out=r[:, t, :], in_=acc[:], func=ACT.Sigmoid, bias=br[:, t:t + 1], scale=1.0)
-            r_of[g] = r
+                bank = psum["gate"].tile([P, GROUP_ROWS], F32, name="g_%d_%d" % (g, t), tag="gate")
+                for o, key in enumerate(("w1", "u1")):
+                    rows = slice(o * GROUP_ROWS, (o + 1) * GROUP_ROWS)
+                    nc.tensor.matmul_mx(
+                        out=bank[:],
+                        lhsT=w_codes[key][:, cols].bitcast(FP8X4), lhsT_scale=w_scales[key][:, cols],
+                        rhs=act_codes[g][:, rows].bitcast(FP8X4), rhs_scale=act_scales[g][:, rows],
+                        start=(o == 0), stop=(o == 1),
+                    )
+                nc.scalar.activation(out=r[:, t, :], in_=bank[:], func=ACT.Sigmoid, bias=bias_gate[:, t:t + 1],
+                                     scale=1.0)
+            gates[g] = r
 
         def reset_state(g):
-            rh = work.tile([P, 4 * GC], BF16, name="rh%d" % g, tag="rh", align_bytes=64)
+            product = work.tile([P, PACK * GROUP_ROWS], BF16, name="reset%d" % g, tag="reset", align_bytes=64)
             nc.vector.tensor_tensor(
-                out=rh[:].rearrange("q (b i t) -> q b t i", i=4, t=4),
-                in0=r_of[g][:].rearrange("q t (b i) -> q b t i", i=4),
-                in1=grp[("h", g)][:].rearrange("q (b i t) -> q b t i", i=4, t=4),
+                out=product[:].rearrange("q (b i t) -> q b t i", i=4, t=PACK),
+                in0=gates[g][:].rearrange("q t (b i) -> q b t i", i=4),
+                in1=acts[g][:, PACK * GROUP_ROWS:].rearrange("q (b i t) -> q b t i", i=4, t=PACK),
                 op=ALU.mult,
             )
-            rh_of[g] = rh
+            resets[g] = product
 
-        def candidate_sum(i, bank):
-            g, j = divmod(i, GT)
+        def quantise_reset_state(g):
+            codes = keep.tile([P, GROUP_ROWS], U32, name="reset_codes%d" % g, align_bytes=64)
+            scales = keep.tile([P, GROUP_ROWS], U8, name="reset_scales%d" % g, align_bytes=64)
+            nc.vector.quantize_mx(out=codes[:].bitcast(FP8X4), scales=scales[:], in_=resets[g][:])
+            reset_codes[g] = codes
+            reset_scales[g] = scales
+
+        def candidate_sum(i, role):
+            g, j = divmod(i, GROUP_TILES)
             if j == 0:
-                o_of[g] = work.tile([P, GT, FEAT], F32, name="o%d" % g, tag="o", bufs=4)
-            cols = slice(j * P, (j + 1) * P)
-            acc = psum[bank].tile([P, FEAT], F32, name="m2_%d" % i, tag=bank)
+                results[g] = work.tile([P, GROUP_TILES, FEAT], F32, name="result%d" % g, tag="result", bufs=3)
+            rows = slice(j * P, (j + 1) * P)
+            bank = psum[role].tile([P, FEAT], F32, name="c_%d" % i, tag=role)
             nc.tensor.matmul_mx(
-                out=acc[:],
-                lhsT=codes[("x", g)][:, cols].bitcast(FP8X4), lhsT_scale=planes[("x", g)][:, cols],
-                rhs=wc["w3"][:].bitcast(FP8X4), rhs_scale=ws["w3"][:],
+                out=bank[:],
+                lhsT=act_codes[g][:, rows].bitcast(FP8X4), lhsT_scale=act_scales[g][:, rows],
+                rhs=w_codes["w3"][:].bitcast(FP8X4), rhs_scale=w_scales["w3"][:],
                 start=True, stop=False,
             )
             nc.tensor.matmul_mx(
-                out=acc[:],
-                lhsT=codes[("rh", g)][:, cols].bitcast(FP8X4), lhsT_scale=planes[("rh", g)][:, cols],
-                rhs=wc["u3"][:].bitcast(FP8X4), rhs_scale=ws["u3"][:],
+                out=bank[:],
+                lhsT=reset_codes[g][:, rows].bitcast(FP8X4), lhsT_scale=reset_scales[g][:, rows],
+                rhs=w_codes["u3"][:].bitcast(FP8X4), rhs_scale=w_scales["u3"][:],
                 start=False, stop=True,
             )
-            nc.vector.tensor_tensor(out=o_of[g][:, j, :], in0=acc[:], in1=bu[:], op=ALU.add)
+            nc.vector.tensor_tensor(out=results[g][:, j, :], in0=bank[:], in1=bias_rows[:], op=ALU.add)
 
         def finish(i):
-            g, j = divmod(i, GT)
-            o = o_of[g]
-            nc.scalar.activation(out=o[:, j, :], in_=o[:, j, :], func=ACT.Tanh)
-            if i >= TILES - FINE_LAST:
-                nc.sync.dma_start(out=o_v[:, i:i + 1, :], in_=o[:, j:j + 1, :])
+            g, j = divmod(i, GROUP_TILES)
+            result = results[g]
+            nc.scalar.activation(out=result[:, j, :], in_=result[:, j, :], func=ACT.Tanh)
+            if i >= TILES - SINGLE_STORES:
+                nc.sync.dma_start(out=out_rows[:, i:i + 1, :], in_=result[:, j:j + 1, :])
             elif j % 2 == 1:
-                nc.sync.dma_start(out=o_v[:, i - 1:i + 1, :], in_=o[:, j - 1:j + 1, :])
+                nc.sync.dma_start(out=out_rows[:, i - 1:i + 1, :], in_=result[:, j - 1:j + 1, :])
 
-        brb = const.tile([P, 4], BF16, name="brb", tag="brb")
+        bias_gate_bf = keep.tile([P, CHUNKS], BF16, name="bias_gate_bf")
         nc.scalar.dma_start(
-            out=brb[:].rearrange("q (u e) -> q u e", u=2),
+            out=bias_gate_bf[:].rearrange("q (u e) -> q u e", u=2),
             in_=bias_r.rearrange("o (u q e) -> q (o u) e", u=2, e=2),
         )
-        bz = const.tile([P, FEAT], BF16, name="bz", tag="bz")
-        nc.gpsimd.memset(bz[:], 0.0)
-        nc.scalar.dma_start(out=bz[0:1, :], in_=bias_u)
-        ident = const.tile([P, P], F32, name="ident", tag="ident")
-        make_identity(nc, ident[:])
-        ones = const.tile([P, P], BF16, name="ones", tag="ones")
+        bias_row = keep.tile([P, FEAT], BF16, name="bias_row")
+        nc.gpsimd.memset(bias_row[:], 0.0)
+        nc.scalar.dma_start(out=bias_row[0:1, :], in_=bias_u)
+        identity = keep.tile([P, P], F32, name="identity")
+        make_identity(nc, identity[:])
+        ones = keep.tile([P, P], BF16, name="ones")
         nc.gpsimd.memset(ones[:], 1.0)
-        bu = const.tile([P, FEAT], F32, name="bu", tag="bu")
+        bias_rows = keep.tile([P, FEAT], F32, name="bias_rows")
 
-        load_w("w1", w1)
-        load_a("x", 0, 2)
-        load_w("u1", u1)
-        load_a("h", 0, 2)
-        load_a("x", 1)
-        load_a("h", 1)
-        load_w("w3", w3)
-        load_w("u3", u3)
-        for g in range(2, NAT_BUFS):
-            load_a("x", g)
-            load_a("h", g)
+        load_weight("w1", w1)
+        load_rows("x", 0, pieces=2)
+        load_weight("u1", u1)
+        load_rows("h", 0, pieces=2)
+        load_rows("x", 1)
+        load_rows("h", 1)
+        load_weight("w3", w3)
+        load_weight("u3", u3)
+        for g in range(2, LOADS_AHEAD):
+            load_rows("x", g)
+            load_rows("h", g)
 
-        regroup_w("w1", True)
-        quantise_w("w1", 2)
-        br = const.tile([P, 4], F32, name="br", tag="br")
-        nc.vector.tensor_copy(out=br[:], in_=brb[:])
-        regroup_w("u1", True)
-        quantise_w("u1", 2)
+        regroup_weight("w1", stationary=True)
+        quantise_weight("w1", pieces=2)
+        bias_gate = keep.tile([P, CHUNKS], F32, name="bias_gate")
+        nc.vector.tensor_copy(out=bias_gate[:], in_=bias_gate_bf[:])
+        regroup_weight("u1", stationary=True)
+        quantise_weight("u1", pieces=2)
         for g in range(LEAD):
-            front(g)
-        early = 0
-        for n in range(G):
+            transpose_group(g)
+
+        filled = 0
+        for n in range(GROUPS):
             gate(n)
             if n == 0:
-                bu_ps = psum["m2"].tile([P, FEAT], F32, name="bu_ps", tag="m2")
-                nc.tensor.matmul(out=bu_ps[:], lhsT=ones[:], rhs=bz[:], start=True, stop=True)
-                nc.scalar.copy(out=bu[:], in_=bu_ps[:])
-                regroup_w("w3", False)
-                regroup_w("u3", False)
-                quantise_w("w3", 1)
-                quantise_w("u3", 1)
+                bank = psum["candidate"].tile([P, FEAT], F32, name="bias_bank", tag="candidate")
+                nc.tensor.matmul(out=bank[:], lhsT=ones[:], rhs=bias_row[:], start=True, stop=True)
+                nc.scalar.copy(out=bias_rows[:], in_=bank[:])
+                regroup_weight("w3", stationary=False)
+                regroup_weight("u3", stationary=False)
+                quantise_weight("w3", pieces=1)
+                quantise_weight("u3", pieces=1)
             if n >= 1:
                 reset_state(n - 1)
-            if n >= FIRST_EARLY:
-                candidate_sum(early, "m2")
-                early += 1
+            if n >= FIRST_FILLED:
+                candidate_sum(filled, "candidate")
+                filled += 1
             if n >= 1:
-                quantise("rh", n - 1, rh_of[n - 1], True)
-            if n + LEAD < G:
-                front(n + LEAD)
-        reset_state(G - 1)
-        for i in range(early):
+                quantise_reset_state(n - 1)
+            if n + LEAD < GROUPS:
+                transpose_group(n + LEAD)
+
+        reset_state(GROUPS - 1)
+        for i in range(filled):
             finish(i)
-        for i in range(early, TILES):
-            candidate_sum(i, BANKS[(i - early) % len(BANKS)])
-            if i == early:
-                quantise("rh", G - 1, rh_of[G - 1], True)
+        for i in range(filled, TILES):
+            candidate_sum(i, TURNS[(i - filled) % len(TURNS)])
+            if i == filled:
+                quantise_reset_state(GROUPS - 1)
             finish(i)

@@ -24,7 +24,7 @@ WORDS = FEAT // 2
 FLOPS = 4 * 2 * ROWS * FEAT * FEAT
 
 LEAD = 2
-LOADS_AHEAD = 4
+LOADS_AHEAD = 5
 FIRST_FILLED = 2
 SINGLE_STORES = 2
 BANKS = {"transposes": 3, "gate": 3, "candidate": 2}
@@ -108,11 +108,11 @@ def tile_grulrcell_pa_t_kernel(tc, x_in, h_in, w1, w3, u1, u3, bias_r, bias_u, o
             w_scales[key] = scales
 
         def transpose_group(g):
-            grouped = work.tile([P, 2 * PACK * GROUP_ROWS], BF16, name="acts%d" % g, tag="acts", bufs=LEAD + 2,
-                                align_bytes=64)
-            words = grouped[:].bitcast(F32).rearrange("q (o b r u) -> q o b r u", o=2, b=2, u=2)
-            for o, key in enumerate(("x", "h")):
+            for key, bufs in (("x", LEAD + 1), ("h", LEAD + 2)):
                 src = loaded[(key, g)][:].bitcast(F32)
+                grouped = work.tile([P, PACK * GROUP_ROWS], BF16, name="acts_%s%d" % (key, g), tag="acts_" + key,
+                                    bufs=bufs, align_bytes=64)
+                words = grouped[:].bitcast(F32).rearrange("q (b r u) -> q b r u", b=2, u=2)
                 for b in range(2):
                     bank = psum["transposes"].tile([P, 2, 2 * P], F32, name="t_%s%d_%d" % (key, g, b),
                                                    tag="transposes")
@@ -124,13 +124,20 @@ def tile_grulrcell_pa_t_kernel(tc, x_in, h_in, w1, w3, u1, u3, bias_r, bias_u, o
                                 src[:, first + u * P:first + (u + 1) * P],
                                 identity[:],
                             )
-                    nc.scalar.copy(out=words[:, o, b], in_=bank[:].rearrange("q u r -> q r u"))
-            codes = keep.tile([P, 2 * GROUP_ROWS], U32, name="act_codes%d" % g, align_bytes=64)
-            scales = keep.tile([P, 2 * GROUP_ROWS], U8, name="act_scales%d" % g, align_bytes=64)
-            nc.vector.quantize_mx(out=codes[:].bitcast(FP8X4), scales=scales[:], in_=grouped[:])
-            acts[g] = grouped
-            act_codes[g] = codes
-            act_scales[g] = scales
+                    nc.scalar.copy(out=words[:, b], in_=bank[:].rearrange("q u r -> q r u"))
+                acts[(key, g)] = grouped
+            for key in ("x", "h"):
+                if key == "x":
+                    codes = keep.tile([P, GROUP_ROWS], U32, name="x_codes%d" % g, align_bytes=64)
+                    scales = keep.tile([P, GROUP_ROWS], U8, name="x_scales%d" % g, align_bytes=64)
+                else:
+                    codes = work.tile([P, GROUP_ROWS], U32, name="h_codes%d" % g, tag="h_codes", bufs=LEAD + 1,
+                                      align_bytes=64)
+                    scales = work.tile([P, GROUP_ROWS], U8, name="h_scales%d" % g, tag="h_scales", bufs=LEAD + 1,
+                                       align_bytes=64)
+                nc.vector.quantize_mx(out=codes[:].bitcast(FP8X4), scales=scales[:], in_=acts[(key, g)][:])
+                act_codes[(key, g)] = codes
+                act_scales[(key, g)] = scales
             if g + LOADS_AHEAD < GROUPS:
                 load_rows("x", g + LOADS_AHEAD)
                 load_rows("h", g + LOADS_AHEAD)
@@ -140,13 +147,12 @@ def tile_grulrcell_pa_t_kernel(tc, x_in, h_in, w1, w3, u1, u3, bias_r, bias_u, o
             for t in range(CHUNKS):
                 cols = slice(t * P, (t + 1) * P)
                 bank = psum["gate"].tile([P, GROUP_ROWS], F32, name="g_%d_%d" % (g, t), tag="gate")
-                for o, key in enumerate(("w1", "u1")):
-                    rows = slice(o * GROUP_ROWS, (o + 1) * GROUP_ROWS)
+                for weight, key in (("w1", "x"), ("u1", "h")):
                     nc.tensor.matmul_mx(
                         out=bank[:],
-                        lhsT=w_codes[key][:, cols].bitcast(FP8X4), lhsT_scale=w_scales[key][:, cols],
-                        rhs=act_codes[g][:, rows].bitcast(FP8X4), rhs_scale=act_scales[g][:, rows],
-                        start=(o == 0), stop=(o == 1),
+                        lhsT=w_codes[weight][:, cols].bitcast(FP8X4), lhsT_scale=w_scales[weight][:, cols],
+                        rhs=act_codes[(key, g)][:].bitcast(FP8X4), rhs_scale=act_scales[(key, g)][:],
+                        start=(key == "x"), stop=(key == "h"),
                     )
                 nc.scalar.activation(out=r[:, t, :], in_=bank[:], func=ACT.Sigmoid, bias=bias_gate[:, t:t + 1],
                                      scale=1.0)
@@ -157,7 +163,7 @@ def tile_grulrcell_pa_t_kernel(tc, x_in, h_in, w1, w3, u1, u3, bias_r, bias_u, o
             nc.vector.tensor_tensor(
                 out=product[:].rearrange("q (b i t) -> q b t i", i=4, t=PACK),
                 in0=gates[g][:].rearrange("q t (b i) -> q b t i", i=4),
-                in1=acts[g][:, PACK * GROUP_ROWS:].rearrange("q (b i t) -> q b t i", i=4, t=PACK),
+                in1=acts[("h", g)][:].rearrange("q (b i t) -> q b t i", i=4, t=PACK),
                 op=ALU.mult,
             )
             resets[g] = product
@@ -172,12 +178,12 @@ def tile_grulrcell_pa_t_kernel(tc, x_in, h_in, w1, w3, u1, u3, bias_r, bias_u, o
         def candidate_sum(i, role):
             g, j = divmod(i, GROUP_TILES)
             if j == 0:
-                results[g] = work.tile([P, GROUP_TILES, FEAT], F32, name="result%d" % g, tag="result", bufs=3)
+                results[g] = work.tile([P, GROUP_TILES, FEAT], F32, name="result%d" % g, tag="result", bufs=4)
             rows = slice(j * P, (j + 1) * P)
             bank = psum[role].tile([P, FEAT], F32, name="c_%d" % i, tag=role)
             nc.tensor.matmul_mx(
                 out=bank[:],
-                lhsT=act_codes[g][:, rows].bitcast(FP8X4), lhsT_scale=act_scales[g][:, rows],
+                lhsT=act_codes[("x", g)][:, rows].bitcast(FP8X4), lhsT_scale=act_scales[("x", g)][:, rows],
                 rhs=w_codes["w3"][:].bitcast(FP8X4), rhs_scale=w_scales["w3"][:],
                 start=True, stop=False,
             )

@@ -23,10 +23,12 @@ CHUNKS = FEAT // P
 WORDS = FEAT // 2
 FLOPS = 4 * 2 * ROWS * FEAT * FEAT
 
+RUN = 4
 LEAD = 2
 LOADS_AHEAD = 5
 FIRST_FILLED = 2
 SINGLE_STORES = 2
+RESULT_TILES = 4
 BANKS = {"transposes": 3, "gate": 3, "candidate": 2}
 TURNS = ("candidate",) * 2 + ("transposes",) * 3 + ("gate",) * 3
 
@@ -39,13 +41,12 @@ def tile_grulrcell_pa_t_kernel(tc, x_in, h_in, w1, w3, u1, u3, bias_r, bias_u, o
         psum = {}
         for role in BANKS:
             psum[role] = ctx.enter_context(tc.psum_pool(name=role, bufs=BANKS[role]))
-        ctx.enter_context(tc.manual_schedule())
 
         rows_of = {
-            "x": x_in.rearrange("(p t) k -> p t k", t=TILES),
-            "h": h_in.rearrange("(p t) k -> p t k", t=TILES),
+            "x": x_in.rearrange("(p i) k -> p i k", i=TILES),
+            "h": h_in.rearrange("(p i) k -> p i k", i=TILES),
         }
-        out_rows = out.rearrange("(p t) n -> p t n", t=TILES)
+        out_rows = out.rearrange("(p i) n -> p i n", i=TILES)
 
         w_loaded = {}
         w_grouped = {}
@@ -61,73 +62,74 @@ def tile_grulrcell_pa_t_kernel(tc, x_in, h_in, w1, w3, u1, u3, bias_r, bias_u, o
         reset_scales = {}
         results = {}
 
-        def load_weight(key, src):
-            t = keep.tile([P, PACK, FEAT], BF16, name="w_loaded_" + key)
+        def load_weight(weight, src):
+            raw = keep.tile([P, PACK, FEAT], BF16, name="w_loaded_" + weight)
             nc.sync.dma_start(
-                out=t[:].rearrange("q (u e) n -> q u (e n)", u=2),
+                out=raw[:].rearrange("q (u e) n -> q u (e n)", u=2),
                 in_=src.rearrange("(u q e) n -> q u (e n)", u=2, e=2),
             )
-            w_loaded[key] = t
+            w_loaded[weight] = raw
 
-        def load_rows(key, g, pieces=1):
-            t = work.tile([P, GROUP_TILES * FEAT], BF16, name="loaded_%s%d" % (key, g), tag="loaded_" + key,
-                          bufs=LOADS_AHEAD)
-            n = GROUP_TILES // pieces
-            for i in range(pieces):
+        def load_rows(operand, g, pieces=1):
+            raw = work.tile([P, GROUP_TILES * FEAT], BF16, name="loaded_%s%d" % (operand, g),
+                            tag="loaded_" + operand, bufs=LOADS_AHEAD)
+            size = GROUP_TILES // pieces
+            for part in range(pieces):
                 nc.sync.dma_start(
-                    out=t[:, i * n * FEAT:(i + 1) * n * FEAT].rearrange("p (j k) -> p j k", j=n),
-                    in_=rows_of[key][:, g * GROUP_TILES + i * n:g * GROUP_TILES + (i + 1) * n, :],
+                    out=raw[:, part * size * FEAT:(part + 1) * size * FEAT].rearrange("p (j k) -> p j k", j=size),
+                    in_=rows_of[operand][:, g * GROUP_TILES + part * size:g * GROUP_TILES + (part + 1) * size, :],
                 )
-            loaded[(key, g)] = t
+            loaded[(operand, g)] = raw
 
-        def regroup_weight(key, stationary):
-            grouped = work.tile([P, PACK * FEAT], BF16, name="w_grouped_" + key, tag="w_grouped", align_bytes=64)
+        def regroup_weight(weight, stationary):
+            grouped = work.tile([P, PACK * FEAT], BF16, name="w_grouped_" + weight, tag="w_grouped",
+                                align_bytes=64)
             if stationary:
-                src = w_loaded[key][:].rearrange("q t (u m e) -> q u e m t", u=2, e=2)
+                src = w_loaded[weight][:].rearrange("q t (u m e) -> q u e m t", u=2, e=2)
                 dst = grouped[:].rearrange("q (u e m t) -> q u e m t", u=2, e=2, t=PACK)
                 for u in range(2):
                     nc.vector.tensor_copy(out=dst[:, u], in_=src[:, u])
             else:
                 nc.vector.tensor_copy(
-                    out=grouped[:].rearrange("q (c i t) -> q c t i", i=4, t=PACK),
-                    in_=w_loaded[key][:].rearrange("q t (c i) -> q c t i", i=4),
+                    out=grouped[:].rearrange("q (b s t) -> q b t s", s=RUN, t=PACK),
+                    in_=w_loaded[weight][:].rearrange("q t (b s) -> q b t s", s=RUN),
                 )
-            w_grouped[key] = grouped
+            w_grouped[weight] = grouped
 
-        def quantise_weight(key, pieces):
-            codes = keep.tile([P, FEAT], U32, name="w_codes_" + key, align_bytes=64)
-            scales = keep.tile([P, FEAT], U8, name="w_scales_" + key, align_bytes=64)
-            n = FEAT // pieces
-            for i in range(pieces):
+        def quantise_weight(weight, pieces):
+            codes = keep.tile([P, FEAT], U32, name="w_codes_" + weight, align_bytes=64)
+            scales = keep.tile([P, FEAT], U8, name="w_scales_" + weight, align_bytes=64)
+            size = FEAT // pieces
+            for part in range(pieces):
                 nc.vector.quantize_mx(
-                    out=codes[:, i * n:(i + 1) * n].bitcast(FP8X4),
-                    scales=scales[:, i * n:(i + 1) * n],
-                    in_=w_grouped[key][:, PACK * i * n:PACK * (i + 1) * n],
+                    out=codes[:, part * size:(part + 1) * size].bitcast(FP8X4),
+                    scales=scales[:, part * size:(part + 1) * size],
+                    in_=w_grouped[weight][:, PACK * part * size:PACK * (part + 1) * size],
                 )
-            w_codes[key] = codes
-            w_scales[key] = scales
+            w_codes[weight] = codes
+            w_scales[weight] = scales
 
         def transpose_group(g):
-            for key, bufs in (("x", LEAD + 1), ("h", LEAD + 2)):
-                src = loaded[(key, g)][:].bitcast(F32)
-                grouped = work.tile([P, PACK * GROUP_ROWS], BF16, name="acts_%s%d" % (key, g), tag="acts_" + key,
-                                    bufs=bufs, align_bytes=64)
-                words = grouped[:].bitcast(F32).rearrange("q (b r u) -> q b r u", b=2, u=2)
-                for b in range(2):
-                    bank = psum["transposes"].tile([P, 2, 2 * P], F32, name="t_%s%d_%d" % (key, g, b),
+            for operand, bufs in (("x", LEAD + 1), ("h", LEAD + 2)):
+                src = loaded[(operand, g)][:].bitcast(F32)
+                grouped = work.tile([P, PACK * GROUP_ROWS], BF16, name="acts_%s%d" % (operand, g),
+                                    tag="acts_" + operand, bufs=bufs, align_bytes=64)
+                words = grouped[:].bitcast(F32).rearrange("q (v w u) -> q v w u", v=2, u=2)
+                for v in range(2):
+                    bank = psum["transposes"].tile([P, 2, 2 * P], F32, name="t_%s%d_%d" % (operand, g, v),
                                                    tag="transposes")
                     for j in range(2):
-                        first = (2 * b + j) * WORDS
+                        first = (2 * v + j) * WORDS
                         for u in range(2):
                             nc.tensor.transpose(
                                 bank[:, u, j * P:(j + 1) * P],
                                 src[:, first + u * P:first + (u + 1) * P],
                                 identity[:],
                             )
-                    nc.scalar.copy(out=words[:, b], in_=bank[:].rearrange("q u r -> q r u"))
-                acts[(key, g)] = grouped
-            for key in ("x", "h"):
-                if key == "x":
+                    nc.scalar.copy(out=words[:, v], in_=bank[:].rearrange("q u w -> q w u"))
+                acts[(operand, g)] = grouped
+            for operand in ("x", "h"):
+                if operand == "x":
                     codes = keep.tile([P, GROUP_ROWS], U32, name="x_codes%d" % g, align_bytes=64)
                     scales = keep.tile([P, GROUP_ROWS], U8, name="x_scales%d" % g, align_bytes=64)
                 else:
@@ -135,9 +137,9 @@ def tile_grulrcell_pa_t_kernel(tc, x_in, h_in, w1, w3, u1, u3, bias_r, bias_u, o
                                       align_bytes=64)
                     scales = work.tile([P, GROUP_ROWS], U8, name="h_scales%d" % g, tag="h_scales", bufs=LEAD + 1,
                                        align_bytes=64)
-                nc.vector.quantize_mx(out=codes[:].bitcast(FP8X4), scales=scales[:], in_=acts[(key, g)][:])
-                act_codes[(key, g)] = codes
-                act_scales[(key, g)] = scales
+                nc.vector.quantize_mx(out=codes[:].bitcast(FP8X4), scales=scales[:], in_=acts[(operand, g)][:])
+                act_codes[(operand, g)] = codes
+                act_scales[(operand, g)] = scales
             if g + LOADS_AHEAD < GROUPS:
                 load_rows("x", g + LOADS_AHEAD)
                 load_rows("h", g + LOADS_AHEAD)
@@ -147,12 +149,12 @@ def tile_grulrcell_pa_t_kernel(tc, x_in, h_in, w1, w3, u1, u3, bias_r, bias_u, o
             for t in range(CHUNKS):
                 cols = slice(t * P, (t + 1) * P)
                 bank = psum["gate"].tile([P, GROUP_ROWS], F32, name="g_%d_%d" % (g, t), tag="gate")
-                for weight, key in (("w1", "x"), ("u1", "h")):
+                for weight, operand in (("w1", "x"), ("u1", "h")):
                     nc.tensor.matmul_mx(
                         out=bank[:],
                         lhsT=w_codes[weight][:, cols].bitcast(FP8X4), lhsT_scale=w_scales[weight][:, cols],
-                        rhs=act_codes[(key, g)][:].bitcast(FP8X4), rhs_scale=act_scales[(key, g)][:],
-                        start=(key == "x"), stop=(key == "h"),
+                        rhs=act_codes[(operand, g)][:].bitcast(FP8X4), rhs_scale=act_scales[(operand, g)][:],
+                        start=(operand == "x"), stop=(operand == "h"),
                     )
                 nc.scalar.activation(out=r[:, t, :], in_=bank[:], func=ACT.Sigmoid, bias=bias_gate[:, t:t + 1],
                                      scale=1.0)
@@ -161,9 +163,9 @@ def tile_grulrcell_pa_t_kernel(tc, x_in, h_in, w1, w3, u1, u3, bias_r, bias_u, o
         def reset_state(g):
             product = work.tile([P, PACK * GROUP_ROWS], BF16, name="reset%d" % g, tag="reset", align_bytes=64)
             nc.vector.tensor_tensor(
-                out=product[:].rearrange("q (b i t) -> q b t i", i=4, t=PACK),
-                in0=gates[g][:].rearrange("q t (b i) -> q b t i", i=4),
-                in1=acts[("h", g)][:].rearrange("q (b i t) -> q b t i", i=4, t=PACK),
+                out=product[:].rearrange("q (b s t) -> q b t s", s=RUN, t=PACK),
+                in0=gates[g][:].rearrange("q t (b s) -> q b t s", s=RUN),
+                in1=acts[("h", g)][:].rearrange("q (b s t) -> q b t s", s=RUN, t=PACK),
                 op=ALU.mult,
             )
             resets[g] = product
@@ -178,7 +180,8 @@ def tile_grulrcell_pa_t_kernel(tc, x_in, h_in, w1, w3, u1, u3, bias_r, bias_u, o
         def candidate_sum(i, role):
             g, j = divmod(i, GROUP_TILES)
             if j == 0:
-                results[g] = work.tile([P, GROUP_TILES, FEAT], F32, name="result%d" % g, tag="result", bufs=4)
+                results[g] = work.tile([P, GROUP_TILES, FEAT], F32, name="result%d" % g, tag="result",
+                                       bufs=RESULT_TILES)
             rows = slice(j * P, (j + 1) * P)
             bank = psum[role].tile([P, FEAT], F32, name="c_%d" % i, tag=role)
             nc.tensor.matmul_mx(
@@ -240,9 +243,9 @@ def tile_grulrcell_pa_t_kernel(tc, x_in, h_in, w1, w3, u1, u3, bias_r, bias_u, o
             transpose_group(g)
 
         filled = 0
-        for n in range(GROUPS):
-            gate(n)
-            if n == 0:
+        for step in range(GROUPS):
+            gate(step)
+            if step == 0:
                 bank = psum["candidate"].tile([P, FEAT], F32, name="bias_bank", tag="candidate")
                 nc.tensor.matmul(out=bank[:], lhsT=ones[:], rhs=bias_row[:], start=True, stop=True)
                 nc.scalar.copy(out=bias_rows[:], in_=bank[:])
@@ -250,15 +253,15 @@ def tile_grulrcell_pa_t_kernel(tc, x_in, h_in, w1, w3, u1, u3, bias_r, bias_u, o
                 regroup_weight("u3", stationary=False)
                 quantise_weight("w3", pieces=1)
                 quantise_weight("u3", pieces=1)
-            if n >= 1:
-                reset_state(n - 1)
-            if n >= FIRST_FILLED:
+            if step >= 1:
+                reset_state(step - 1)
+            if step >= FIRST_FILLED:
                 candidate_sum(filled, "candidate")
                 filled += 1
-            if n >= 1:
-                quantise_reset_state(n - 1)
-            if n + LEAD < GROUPS:
-                transpose_group(n + LEAD)
+            if step >= 1:
+                quantise_reset_state(step - 1)
+            if step + LEAD < GROUPS:
+                transpose_group(step + LEAD)
 
         reset_state(GROUPS - 1)
         for i in range(filled):

from contextlib import ExitStack

import concourse.mybir as mybir
from concourse.masks import make_identity

F32 = mybir.dt.float32
BF16 = mybir.dt.bfloat16
U32 = mybir.dt.uint32
U8 = mybir.dt.uint8
FP8X4 = mybir.dt.float8_e4m3fn_x4
ACT = mybir.ActivationFunctionType
ALU = mybir.AluOpType

P = 128
PACK = 4
ROWS = 4096
FEAT = 512
TILES = ROWS // P
GROUP_TILES = 4
GROUPS = TILES // GROUP_TILES
GROUP_ROWS = GROUP_TILES * P
CHUNKS = FEAT // P
WORDS = FEAT // 2
FLOPS = 4 * 2 * ROWS * FEAT * FEAT

RUN = 4
LEAD = 2
LOADS_AHEAD = 5
FIRST_FILLED = 2
SINGLE_STORES = 2
RESULT_TILES = 4
BANKS = {"transposes": 3, "gate": 3, "candidate": 2}
TURNS = ("candidate",) * 2 + ("transposes",) * 3 + ("gate",) * 3


def tile_grulrcell_pa_t_kernel(tc, x_in, h_in, w1, w3, u1, u3, bias_r, bias_u, out):
    nc = tc.nc
    with ExitStack() as ctx:
        keep = ctx.enter_context(tc.tile_pool(name="keep", bufs=1))
        work = ctx.enter_context(tc.tile_pool(name="work", bufs=2))
        psum = {}
        for role in BANKS:
            psum[role] = ctx.enter_context(tc.psum_pool(name=role, bufs=BANKS[role]))

        rows_of = {
            "x": x_in.rearrange("(p i) k -> p i k", i=TILES),
            "h": h_in.rearrange("(p i) k -> p i k", i=TILES),
        }
        out_rows = out.rearrange("(p i) n -> p i n", i=TILES)

        w_loaded = {}
        w_grouped = {}
        w_codes = {}
        w_scales = {}
        loaded = {}
        acts = {}
        act_codes = {}
        act_scales = {}
        gates = {}
        resets = {}
        reset_codes = {}
        reset_scales = {}
        results = {}

        def load_weight(weight, src):
            raw = keep.tile([P, PACK, FEAT], BF16, name="w_loaded_" + weight)
            nc.sync.dma_start(
                out=raw[:].rearrange("q (u e) n -> q u (e n)", u=2),
                in_=src.rearrange("(u q e) n -> q u (e n)", u=2, e=2),
            )
            w_loaded[weight] = raw

        def load_rows(operand, g, pieces=1):
            raw = work.tile([P, GROUP_TILES * FEAT], BF16, name="loaded_%s%d" % (operand, g),
                            tag="loaded_" + operand, bufs=LOADS_AHEAD)
            size = GROUP_TILES // pieces
            for part in range(pieces):
                nc.sync.dma_start(
                    out=raw[:, part * size * FEAT:(part + 1) * size * FEAT].rearrange("p (j k) -> p j k", j=size),
                    in_=rows_of[operand][:, g * GROUP_TILES + part * size:g * GROUP_TILES + (part + 1) * size, :],
                )
            loaded[(operand, g)] = raw

        def regroup_weight(weight, stationary):
            grouped = work.tile([P, PACK * FEAT], BF16, name="w_grouped_" + weight, tag="w_grouped",
                                align_bytes=64)
            if stationary:
                src = w_loaded[weight][:].rearrange("q t (u m e) -> q u e m t", u=2, e=2)
                dst = grouped[:].rearrange("q (u e m t) -> q u e m t", u=2, e=2, t=PACK)
                for u in range(2):
                    nc.vector.tensor_copy(out=dst[:, u], in_=src[:, u])
            else:
                nc.vector.tensor_copy(
                    out=grouped[:].rearrange("q (b s t) -> q b t s", s=RUN, t=PACK),
                    in_=w_loaded[weight][:].rearrange("q t (b s) -> q b t s", s=RUN),
                )
            w_grouped[weight] = grouped

        def quantise_weight(weight, pieces):
            codes = keep.tile([P, FEAT], U32, name="w_codes_" + weight, align_bytes=64)
            scales = keep.tile([P, FEAT], U8, name="w_scales_" + weight, align_bytes=64)
            size = FEAT // pieces
            for part in range(pieces):
                nc.vector.quantize_mx(
                    out=codes[:, part * size:(part + 1) * size].bitcast(FP8X4),
                    scales=scales[:, part * size:(part + 1) * size],
                    in_=w_grouped[weight][:, PACK * part * size:PACK * (part + 1) * size],
                )
            w_codes[weight] = codes
            w_scales[weight] = scales

        def transpose_group(g):
            for operand, bufs in (("x", LEAD + 1), ("h", LEAD + 2)):
                src = loaded[(operand, g)][:].bitcast(F32)
                grouped = work.tile([P, PACK * GROUP_ROWS], BF16, name="acts_%s%d" % (operand, g),
                                    tag="acts_" + operand, bufs=bufs, align_bytes=64)
                words = grouped[:].bitcast(F32).rearrange("q (v w u) -> q v w u", v=2, u=2)
                for v in range(2):
                    bank = psum["transposes"].tile([P, 2, 2 * P], F32, name="t_%s%d_%d" % (operand, g, v),
                                                   tag="transposes")
                    for j in range(2):
                        first = (2 * v + j) * WORDS
                        for u in range(2):
                            nc.tensor.transpose(
                                bank[:, u, j * P:(j + 1) * P],
                                src[:, first + u * P:first + (u + 1) * P],
                                identity[:],
                            )
                    nc.scalar.copy(out=words[:, v], in_=bank[:].rearrange("q u w -> q w u"))
                acts[(operand, g)] = grouped
            for operand in ("x", "h"):
                if operand == "x":
                    codes = keep.tile([P, GROUP_ROWS], U32, name="x_codes%d" % g, align_bytes=64)
                    scales = keep.tile([P, GROUP_ROWS], U8, name="x_scales%d" % g, align_bytes=64)
                else:
                    codes = work.tile([P, GROUP_ROWS], U32, name="h_codes%d" % g, tag="h_codes", bufs=LEAD + 1,
                                      align_bytes=64)
                    scales = work.tile([P, GROUP_ROWS], U8, name="h_scales%d" % g, tag="h_scales", bufs=LEAD + 1,
                                       align_bytes=64)
                nc.vector.quantize_mx(out=codes[:].bitcast(FP8X4), scales=scales[:], in_=acts[(operand, g)][:])
                act_codes[(operand, g)] = codes
                act_scales[(operand, g)] = scales
            if g + LOADS_AHEAD < GROUPS:
                load_rows("x", g + LOADS_AHEAD)
                load_rows("h", g + LOADS_AHEAD)

        def gate(g):
            r = work.tile([P, CHUNKS, GROUP_ROWS], F32, name="gate%d" % g, tag="gate")
            for t in range(CHUNKS):
                cols = slice(t * P, (t + 1) * P)
                bank = psum["gate"].tile([P, GROUP_ROWS], F32, name="g_%d_%d" % (g, t), tag="gate")
                for weight, operand in (("w1", "x"), ("u1", "h")):
                    nc.tensor.matmul_mx(
                        out=bank[:],
                        lhsT=w_codes[weight][:, cols].bitcast(FP8X4), lhsT_scale=w_scales[weight][:, cols],
                        rhs=act_codes[(operand, g)][:].bitcast(FP8X4), rhs_scale=act_scales[(operand, g)][:],
                        start=(operand == "x"), stop=(operand == "h"),
                    )
                nc.scalar.activation(out=r[:, t, :], in_=bank[:], func=ACT.Sigmoid, bias=bias_gate[:, t:t + 1],
                                     scale=1.0)
            gates[g] = r

        def reset_state(g):
            product = work.tile([P, PACK * GROUP_ROWS], BF16, name="reset%d" % g, tag="reset", align_bytes=64)
            nc.vector.tensor_tensor(
                out=product[:].rearrange("q (b s t) -> q b t s", s=RUN, t=PACK),
                in0=gates[g][:].rearrange("q t (b s) -> q b t s", s=RUN),
                in1=acts[("h", g)][:].rearrange("q (b s t) -> q b t s", s=RUN, t=PACK),
                op=ALU.mult,
            )
            resets[g] = product

        def quantise_reset_state(g):
            codes = keep.tile([P, GROUP_ROWS], U32, name="reset_codes%d" % g, align_bytes=64)
            scales = keep.tile([P, GROUP_ROWS], U8, name="reset_scales%d" % g, align_bytes=64)
            nc.vector.quantize_mx(out=codes[:].bitcast(FP8X4), scales=scales[:], in_=resets[g][:])
            reset_codes[g] = codes
            reset_scales[g] = scales

        def candidate_sum(i, role):
            g, j = divmod(i, GROUP_TILES)
            if j == 0:
                results[g] = work.tile([P, GROUP_TILES, FEAT], F32, name="result%d" % g, tag="result",
                                       bufs=RESULT_TILES)
            rows = slice(j * P, (j + 1) * P)
            bank = psum[role].tile([P, FEAT], F32, name="c_%d" % i, tag=role)
            nc.tensor.matmul_mx(
                out=bank[:],
                lhsT=act_codes[("x", g)][:, rows].bitcast(FP8X4), lhsT_scale=act_scales[("x", g)][:, rows],
                rhs=w_codes["w3"][:].bitcast(FP8X4), rhs_scale=w_scales["w3"][:],
                start=True, stop=False,
            )
            nc.tensor.matmul_mx(
                out=bank[:],
                lhsT=reset_codes[g][:, rows].bitcast(FP8X4), lhsT_scale=reset_scales[g][:, rows],
                rhs=w_codes["u3"][:].bitcast(FP8X4), rhs_scale=w_scales["u3"][:],
                start=False, stop=True,
            )
            nc.vector.tensor_tensor(out=results[g][:, j, :], in0=bank[:], in1=bias_rows[:], op=ALU.add)

        def finish(i):
            g, j = divmod(i, GROUP_TILES)
            result = results[g]
            nc.scalar.activation(out=result[:, j, :], in_=result[:, j, :], func=ACT.Tanh)
            if i >= TILES - SINGLE_STORES:
                nc.sync.dma_start(out=out_rows[:, i:i + 1, :], in_=result[:, j:j + 1, :])
            elif j % 2 == 1:
                nc.sync.dma_start(out=out_rows[:, i - 1:i + 1, :], in_=result[:, j - 1:j + 1, :])

        bias_gate_bf = keep.tile([P, CHUNKS], BF16, name="bias_gate_bf")
        nc.scalar.dma_start(
            out=bias_gate_bf[:].rearrange("q (u e) -> q u e", u=2),
            in_=bias_r.rearrange("o (u q e) -> q (o u) e", u=2, e=2),
        )
        bias_row = keep.tile([P, FEAT], BF16, name="bias_row")
        nc.gpsimd.memset(bias_row[:], 0.0)
        nc.scalar.dma_start(out=bias_row[0:1, :], in_=bias_u)
        identity = keep.tile([P, P], F32, name="identity")
        make_identity(nc, identity[:])
        ones = keep.tile([P, P], BF16, name="ones")
        nc.gpsimd.memset(ones[:], 1.0)
        bias_rows = keep.tile([P, FEAT], F32, name="bias_rows")

        load_weight("w1", w1)
        load_rows("x", 0, pieces=2)
        load_weight("u1", u1)
        load_rows("h", 0, pieces=2)
        load_rows("x", 1)
        load_rows("h", 1)
        load_weight("w3", w3)
        load_weight("u3", u3)
        for g in range(2, LOADS_AHEAD):
            load_rows("x", g)
            load_rows("h", g)

        regroup_weight("w1", stationary=True)
        quantise_weight("w1", pieces=2)
        bias_gate = keep.tile([P, CHUNKS], F32, name="bias_gate")
        nc.vector.tensor_copy(out=bias_gate[:], in_=bias_gate_bf[:])
        regroup_weight("u1", stationary=True)
        quantise_weight("u1", pieces=2)
        for g in range(LEAD):
            transpose_group(g)

        filled = 0
        for step in range(GROUPS):
            gate(step)
            if step == 0:
                bank = psum["candidate"].tile([P, FEAT], F32, name="bias_bank", tag="candidate")
                nc.tensor.matmul(out=bank[:], lhsT=ones[:], rhs=bias_row[:], start=True, stop=True)
                nc.scalar.copy(out=bias_rows[:], in_=bank[:])
                regroup_weight("w3", stationary=False)
                regroup_weight("u3", stationary=False)
                quantise_weight("w3", pieces=1)
                quantise_weight("u3", pieces=1)
            if step >= 1:
                reset_state(step - 1)
            if step >= FIRST_FILLED:
                candidate_sum(filled, "candidate")
                filled += 1
            if step >= 1:
                quantise_reset_state(step - 1)
            if step + LEAD < GROUPS:
                transpose_group(step + LEAD)

        reset_state(GROUPS - 1)
        for i in range(filled):
            finish(i)
        for i in range(filled, TILES):
            candidate_sum(i, TURNS[(i - filled) % len(TURNS)])
            if i == filled:
                quantise_reset_state(GROUPS - 1)
            finish(i)
